import numpy as np
import ml_dtypes

BF16 = ml_dtypes.bfloat16


def bf(x):
    return np.asarray(x, np.float32).astype(BF16)


def f32(x):
    return np.asarray(x, np.float32)


def f64(x):
    return np.asarray(x).astype(np.float64)


def striped(idx):
    return np.tile(idx.reshape(-1, 16).T, (8, 1))


IN, D, M, S, T, DEG, N = 128, 128, 128, 1024, 512, 16, 8192
NEG_SLOPE = 0.2


def leaky(v):
    return np.maximum(v, NEG_SLOPE * v)


def setup_inputs():
    x_node = bf(np.random.standard_normal((IN, S)))
    w1 = bf(np.random.standard_normal((IN, D)) / np.sqrt(IN))
    b1 = f32(0.1 * np.random.standard_normal((D, 1)))
    w2 = bf(np.random.standard_normal((D, D)) / np.sqrt(D))
    b2 = f32(0.1 * np.random.standard_normal((D, 1)))
    w21 = bf(2.0 * np.random.standard_normal((D, M)) / np.sqrt(D))
    b21 = f32(0.1 * np.random.standard_normal((M, 1)))
    idx = np.concatenate([np.random.permutation(S)[:T] for _ in range(DEG)])
    assert idx.size == N
    return {"x_node": x_node, "w1": w1, "b1": b1, "w2": w2, "b2": b2, "w21": w21, "b21": b21, "offs": striped(idx)}


def reference(x_node, w1, b1, w2, b2, w21, b21, offs):
    idx = offs[:16].T.reshape(-1)
    x1 = leaky(f64(w1).T @ f64(x_node) + f64(b1))
    h = leaky(f64(w2).T @ x1 + f64(b2))
    p = f64(w21).T @ h[:, idx]
    agg = p.reshape(M, DEG, T).sum(axis=1) / DEG
    return leaky(agg + f64(b21))

@@ -1,0 +1,69 @@
+import concourse.mybir as mybir
+
+BF16 = mybir.dt.bfloat16
+F32 = mybir.dt.float32
+U16 = mybir.dt.uint16
+IDENTITY = mybir.ActivationFunctionType.Identity
+MULT = mybir.AluOpType.mult
+MAX = mybir.AluOpType.max
+
+P = 128
+NODES = 1024
+TARGETS = 512
+DEGREE = 16
+NEG_SLOPE = 0.2
+CHUNK = 512
+OFFSET_COLUMNS = TARGETS // 16
+
+FLOPS = 2 * P * P * (2 * NODES + DEGREE * TARGETS)
+
+
+def leaky_affine(nc, work, dest, product, scale, bias):
+    v = work.tile([P, CHUNK], F32)
+    nc.scalar.activation(v[:], product, IDENTITY, bias=bias[:], scale=scale)
+    nc.vector.scalar_tensor_tensor(dest, v[:], NEG_SLOPE, v[:], MULT, MAX)
+
+
+def tile_memlayer_kernel(tc, x_node, w1, b1, w2, b2, w21, b21, offs, out):
+    nc = tc.nc
+    with (
+        tc.tile_pool(name="held", bufs=1) as held,
+        tc.tile_pool(name="work", bufs=2) as work,
+        tc.psum_pool(name="mlp_psum", bufs=2) as mlp_psum,
+        tc.psum_pool(name="sum_psum", bufs=1) as sum_psum,
+    ):
+        x_sb = held.tile([P, NODES], BF16)
+        x1 = held.tile([P, NODES], BF16)
+        h = held.tile([P, NODES], BF16)
+        w1_sb = held.tile([P, P], BF16)
+        w2_sb = held.tile([P, P], BF16)
+        w21_sb = held.tile([P, P], BF16)
+        b1_sb = held.tile([P, 1], F32)
+        b2_sb = held.tile([P, 1], F32)
+        b21_sb = held.tile([P, 1], F32)
+        offsets = held.tile([P, DEGREE * OFFSET_COLUMNS], U16)
+        out_sb = held.tile([P, TARGETS], F32)
+
+        nc.sync.dma_start(x_sb[:, 0:CHUNK], x_node[:, 0:CHUNK])
+        nc.scalar.dma_start(w1_sb[:], w1)
+        nc.scalar.dma_start(x_sb[:, CHUNK:NODES], x_node[:, CHUNK:NODES])
+        nc.sync.dma_start(b1_sb[:], b1)
+        nc.sync.dma_start(w2_sb[:], w2)
+        nc.scalar.dma_start(b2_sb[:], b2)
+        nc.sync.dma_start(offsets[:], offs)
+        nc.scalar.dma_start(w21_sb[:], w21)
+        nc.scalar.dma_start(b21_sb[:], b21)
+
+        for source, weights, bias, dest in ((x_sb, w1_sb, b1_sb, x1), (x1, w2_sb, b2_sb, h)):
+            for c in range(0, NODES, CHUNK):
+                product = mlp_psum.tile([P, CHUNK], F32)
+                nc.tensor.matmul(product[:], weights[:], source[:, c : c + CHUNK])
+                leaky_affine(nc, work, dest[:, c : c + CHUNK], product[:], 1.0, bias)
+
+        total = sum_psum.tile([P, TARGETS], F32)
+        for e in range(DEGREE):
+            neighbours = h[:].indirect(offsets[:, e * OFFSET_COLUMNS : (e + 1) * OFFSET_COLUMNS])
+            nc.tensor.matmul(total[:], w21_sb[:], neighbours, start=(e == 0), stop=(e == DEGREE - 1))
+
+        leaky_affine(nc, work, out_sb[:], total[:], 1.0 / DEGREE, b21_sb)
+        nc.sync.dma_start(out, out_sb[:])

@@ -44,6 +44,10 @@ def tile_memlayer_kernel(tc, x_node, w1, b1, w2, b2, w21, b21, offs, out):
         offsets = held.tile([P, DEGREE * OFFSET_COLUMNS], U16)
         out_sb = held.tile([P, TARGETS], F32)
 
+        one_column = held.tile([P, 1], F32)
+        nc.vector.memset(one_column[:], 0.0)
+        nc.scalar.activation(one_column[:], one_column[:], IDENTITY)
+
         nc.sync.dma_start(x_sb[:, 0:CHUNK], x_node[:, 0:CHUNK])
         nc.scalar.dma_start(w1_sb[:], w1)
         nc.scalar.dma_start(x_sb[:, CHUNK:NODES], x_node[:, CHUNK:NODES])

@@ -12,14 +12,15 @@ NODES = 1024
 TARGETS = 512
 DEGREE = 16
 NEG_SLOPE = 0.2
-CHUNK = 512
+CHUNK = 256
+HALF = NODES // 2
 OFFSET_COLUMNS = TARGETS // 16
 
 FLOPS = 2 * P * P * (2 * NODES + DEGREE * TARGETS)
 
 
 def leaky_affine(nc, work, dest, product, scale, bias):
-    v = work.tile([P, CHUNK], F32)
+    v = work.tile(list(product.shape), F32)
     nc.scalar.activation(v[:], product, IDENTITY, bias=bias[:], scale=scale)
     nc.vector.scalar_tensor_tensor(dest, v[:], NEG_SLOPE, v[:], MULT, MAX)
 
@@ -28,8 +29,8 @@ def tile_memlayer_kernel(tc, x_node, w1, b1, w2, b2, w21, b21, offs, out):
     nc = tc.nc
     with (
         tc.tile_pool(name="held", bufs=1) as held,
-        tc.tile_pool(name="work", bufs=2) as work,
-        tc.psum_pool(name="mlp_psum", bufs=2) as mlp_psum,
+        tc.tile_pool(name="work", bufs=4) as work,
+        tc.psum_pool(name="mlp_psum", bufs=4) as mlp_psum,
         tc.psum_pool(name="sum_psum", bufs=1) as sum_psum,
     ):
         x_sb = held.tile([P, NODES], BF16)
@@ -44,19 +45,19 @@ def tile_memlayer_kernel(tc, x_node, w1, b1, w2, b2, w21, b21, offs, out):
         offsets = held.tile([P, DEGREE * OFFSET_COLUMNS], U16)
         out_sb = held.tile([P, TARGETS], F32)
 
+        nc.sync.dma_start(x_sb[:, 0:HALF], x_node[:, 0:HALF])
+        nc.scalar.dma_start(w1_sb[:], w1)
+        nc.gpsimd.dma_start(b2_sb[:], b2)
+        nc.sync.dma_start(x_sb[:, HALF:NODES], x_node[:, HALF:NODES])
+        nc.scalar.dma_start(b1_sb[:], b1)
+        nc.gpsimd.dma_start(w21_sb[:], w21)
+        nc.sync.dma_start(w2_sb[:], w2)
+        nc.gpsimd.dma_start(b21_sb[:], b21)
+        nc.sync.dma_start(offsets[:], offs)
+
         one_column = held.tile([P, 1], F32)
         nc.vector.memset(one_column[:], 0.0)
         nc.scalar.activation(one_column[:], one_column[:], IDENTITY)
-
-        nc.sync.dma_start(x_sb[:, 0:CHUNK], x_node[:, 0:CHUNK])
-        nc.scalar.dma_start(w1_sb[:], w1)
-        nc.scalar.dma_start(x_sb[:, CHUNK:NODES], x_node[:, CHUNK:NODES])
-        nc.sync.dma_start(b1_sb[:], b1)
-        nc.sync.dma_start(w2_sb[:], w2)
-        nc.scalar.dma_start(b2_sb[:], b2)
-        nc.sync.dma_start(offsets[:], offs)
-        nc.scalar.dma_start(w21_sb[:], w21)
-        nc.scalar.dma_start(b21_sb[:], b21)
 
         for source, weights, bias, dest in ((x_sb, w1_sb, b1_sb, x1), (x1, w2_sb, b2_sb, h)):
             for c in range(0, NODES, CHUNK):

@@ -50,9 +50,9 @@ def tile_memlayer_kernel(tc, x_node, w1, b1, w2, b2, w21, b21, offs, out):
         nc.gpsimd.dma_start(b2_sb[:], b2)
         nc.sync.dma_start(x_sb[:, HALF:NODES], x_node[:, HALF:NODES])
         nc.scalar.dma_start(b1_sb[:], b1)
-        nc.gpsimd.dma_start(w21_sb[:], w21)
-        nc.sync.dma_start(w2_sb[:], w2)
         nc.gpsimd.dma_start(b21_sb[:], b21)
+        nc.sync.dma_start(w2_sb[:], w2)
+        nc.sync.dma_start(w21_sb[:], w21)
         nc.sync.dma_start(offsets[:], offs)
 
         one_column = held.tile([P, 1], F32)
@@ -70,5 +70,6 @@ def tile_memlayer_kernel(tc, x_node, w1, b1, w2, b2, w21, b21, offs, out):
             neighbours = h[:].indirect(offsets[:, e * OFFSET_COLUMNS : (e + 1) * OFFSET_COLUMNS])
             nc.tensor.matmul(total[:], w21_sb[:], neighbours, start=(e == 0), stop=(e == DEGREE - 1))
 
-        leaky_affine(nc, work, out_sb[:], total[:], 1.0 / DEGREE, b21_sb)
-        nc.sync.dma_start(out, out_sb[:])
+        for c, queue in zip(range(0, TARGETS, CHUNK), (nc.sync, nc.scalar)):
+            leaky_affine(nc, work, out_sb[:, c : c + CHUNK], total[:, c : c + CHUNK], 1.0 / DEGREE, b21_sb)
+            queue.dma_start(out[:, c : c + CHUNK], out_sb[:, c : c + CHUNK])

@@ -14,6 +14,8 @@ DEGREE = 16
 NEG_SLOPE = 0.2
 CHUNK = 256
 HALF = NODES // 2
+WARM_COLUMNS = 512
+WARM_MATMULS = 4
 OFFSET_COLUMNS = TARGETS // 16
 
 FLOPS = 2 * P * P * (2 * NODES + DEGREE * TARGETS)
@@ -32,6 +34,7 @@ def tile_memlayer_kernel(tc, x_node, w1, b1, w2, b2, w21, b21, offs, out):
         tc.tile_pool(name="work", bufs=4) as work,
         tc.psum_pool(name="mlp_psum", bufs=4) as mlp_psum,
         tc.psum_pool(name="sum_psum", bufs=1) as sum_psum,
+        tc.psum_pool(name="warm_psum", bufs=1) as warm_psum,
     ):
         x_sb = held.tile([P, NODES], BF16)
         x1 = held.tile([P, NODES], BF16)
@@ -59,6 +62,12 @@ def tile_memlayer_kernel(tc, x_node, w1, b1, w2, b2, w21, b21, offs, out):
         nc.vector.memset(one_column[:], 0.0)
         nc.scalar.activation(one_column[:], one_column[:], IDENTITY)
 
+        zeros = held.tile([P, WARM_COLUMNS], BF16)
+        nc.vector.memset(zeros[:], 0.0)
+        unread = warm_psum.tile([P, WARM_COLUMNS], F32)
+        for repeat in range(WARM_MATMULS):
+            nc.tensor.matmul(unread[:], zeros[:, 0:P], zeros[:])
+
         for source, weights, bias, dest in ((x_sb, w1_sb, b1_sb, x1), (x1, w2_sb, b2_sb, h)):
             for c in range(0, NODES, CHUNK):
                 product = mlp_psum.tile([P, CHUNK], F32)
@@ -70,6 +79,5 @@ def tile_memlayer_kernel(tc, x_node, w1, b1, w2, b2, w21, b21, offs, out):
             neighbours = h[:].indirect(offsets[:, e * OFFSET_COLUMNS : (e + 1) * OFFSET_COLUMNS])
             nc.tensor.matmul(total[:], w21_sb[:], neighbours, start=(e == 0), stop=(e == DEGREE - 1))
 
-        for c, queue in zip(range(0, TARGETS, CHUNK), (nc.sync, nc.scalar)):
-            leaky_affine(nc, work, out_sb[:, c : c + CHUNK], total[:, c : c + CHUNK], 1.0 / DEGREE, b21_sb)
-            queue.dma_start(out[:, c : c + CHUNK], out_sb[:, c : c + CHUNK])
+        leaky_affine(nc, work, out_sb[:], total[:], 1.0 / DEGREE, b21_sb)
+        nc.sync.dma_start(out, out_sb[:])

@@ -12,10 +12,9 @@ NODES = 1024
 TARGETS = 512
 DEGREE = 16
 NEG_SLOPE = 0.2
-CHUNK = 256
+CHUNK = 128
+OUT_CHUNK = 256
 HALF = NODES // 2
-WARM_COLUMNS = 512
-WARM_MATMULS = 4
 OFFSET_COLUMNS = TARGETS // 16
 
 FLOPS = 2 * P * P * (2 * NODES + DEGREE * TARGETS)
@@ -31,10 +30,9 @@ def tile_memlayer_kernel(tc, x_node, w1, b1, w2, b2, w21, b21, offs, out):
     nc = tc.nc
     with (
         tc.tile_pool(name="held", bufs=1) as held,
-        tc.tile_pool(name="work", bufs=4) as work,
-        tc.psum_pool(name="mlp_psum", bufs=4) as mlp_psum,
+        tc.tile_pool(name="work", bufs=6) as work,
+        tc.psum_pool(name="mlp_psum", bufs=6) as mlp_psum,
         tc.psum_pool(name="sum_psum", bufs=1) as sum_psum,
-        tc.psum_pool(name="warm_psum", bufs=1) as warm_psum,
     ):
         x_sb = held.tile([P, NODES], BF16)
         x1 = held.tile([P, NODES], BF16)
@@ -62,12 +60,6 @@ def tile_memlayer_kernel(tc, x_node, w1, b1, w2, b2, w21, b21, offs, out):
         nc.vector.memset(one_column[:], 0.0)
         nc.scalar.activation(one_column[:], one_column[:], IDENTITY)
 
-        zeros = held.tile([P, WARM_COLUMNS], BF16)
-        nc.vector.memset(zeros[:], 0.0)
-        unread = warm_psum.tile([P, WARM_COLUMNS], F32)
-        for repeat in range(WARM_MATMULS):
-            nc.tensor.matmul(unread[:], zeros[:, 0:P], zeros[:])
-
         for source, weights, bias, dest in ((x_sb, w1_sb, b1_sb, x1), (x1, w2_sb, b2_sb, h)):
             for c in range(0, NODES, CHUNK):
                 product = mlp_psum.tile([P, CHUNK], F32)
@@ -79,5 +71,6 @@ def tile_memlayer_kernel(tc, x_node, w1, b1, w2, b2, w21, b21, offs, out):
             neighbours = h[:].indirect(offsets[:, e * OFFSET_COLUMNS : (e + 1) * OFFSET_COLUMNS])
             nc.tensor.matmul(total[:], w21_sb[:], neighbours, start=(e == 0), stop=(e == DEGREE - 1))
 
-        leaky_affine(nc, work, out_sb[:], total[:], 1.0 / DEGREE, b21_sb)
-        nc.sync.dma_start(out, out_sb[:])
+        for c, queue in zip(range(0, TARGETS, OUT_CHUNK), (nc.sync, nc.scalar)):
+            leaky_affine(nc, work, out_sb[:, c : c + OUT_CHUNK], total[:, c : c + OUT_CHUNK], 1.0 / DEGREE, b21_sb)
+            queue.dma_start(out[:, c : c + OUT_CHUNK], out_sb[:, c : c + OUT_CHUNK])

@@ -15,6 +15,7 @@ NEG_SLOPE = 0.2
 CHUNK = 128
 OUT_CHUNK = 256
 HALF = NODES // 2
+WARM_MATMULS = 12
 OFFSET_COLUMNS = TARGETS // 16
 
 FLOPS = 2 * P * P * (2 * NODES + DEGREE * TARGETS)
@@ -33,6 +34,7 @@ def tile_memlayer_kernel(tc, x_node, w1, b1, w2, b2, w21, b21, offs, out):
         tc.tile_pool(name="work", bufs=6) as work,
         tc.psum_pool(name="mlp_psum", bufs=6) as mlp_psum,
         tc.psum_pool(name="sum_psum", bufs=1) as sum_psum,
+        tc.psum_pool(name="warm_psum", bufs=1) as warm_psum,
     ):
         x_sb = held.tile([P, NODES], BF16)
         x1 = held.tile([P, NODES], BF16)
@@ -55,6 +57,12 @@ def tile_memlayer_kernel(tc, x_node, w1, b1, w2, b2, w21, b21, offs, out):
         nc.sync.dma_start(w2_sb[:], w2)
         nc.sync.dma_start(w21_sb[:], w21)
         nc.sync.dma_start(offsets[:], offs)
+
+        zeros = held.tile([P, P], BF16)
+        nc.vector.memset(zeros[:], 0.0)
+        unread = warm_psum.tile([P, P], F32)
+        for repeat in range(WARM_MATMULS):
+            nc.tensor.matmul(unread[:], zeros[:], zeros[:])
 
         one_column = held.tile([P, 1], F32)
         nc.vector.memset(one_column[:], 0.0)

@@ -14,7 +14,6 @@ DEGREE = 16
 NEG_SLOPE = 0.2
 CHUNK = 128
 OUT_CHUNK = 256
-HALF = NODES // 2
 WARM_MATMULS = 12
 OFFSET_COLUMNS = TARGETS // 16
 
@@ -48,14 +47,17 @@ def tile_memlayer_kernel(tc, x_node, w1, b1, w2, b2, w21, b21, offs, out):
         offsets = held.tile([P, DEGREE * OFFSET_COLUMNS], U16)
         out_sb = held.tile([P, TARGETS], F32)
 
-        nc.sync.dma_start(x_sb[:, 0:HALF], x_node[:, 0:HALF])
-        nc.scalar.dma_start(w1_sb[:], w1)
-        nc.gpsimd.dma_start(b2_sb[:], b2)
-        nc.sync.dma_start(x_sb[:, HALF:NODES], x_node[:, HALF:NODES])
-        nc.scalar.dma_start(b1_sb[:], b1)
-        nc.gpsimd.dma_start(b21_sb[:], b21)
+        nc.sync.dma_start(w1_sb[:], w1)
+        nc.sync.dma_start(x_sb[:, 0:CHUNK], x_node[:, 0:CHUNK])
+        nc.sync.dma_start(b1_sb[:], b1)
+        loaded = CHUNK
+        while loaded < NODES:
+            nc.sync.dma_start(x_sb[:, loaded : 2 * loaded], x_node[:, loaded : 2 * loaded])
+            loaded = 2 * loaded
         nc.sync.dma_start(w2_sb[:], w2)
+        nc.sync.dma_start(b2_sb[:], b2)
         nc.sync.dma_start(w21_sb[:], w21)
+        nc.sync.dma_start(b21_sb[:], b21)
         nc.sync.dma_start(offsets[:], offs)
 
         zeros = held.tile([P, P], BF16)

@@ -81,6 +81,6 @@ def tile_memlayer_kernel(tc, x_node, w1, b1, w2, b2, w21, b21, offs, out):
             neighbours = h[:].indirect(offsets[:, e * OFFSET_COLUMNS : (e + 1) * OFFSET_COLUMNS])
             nc.tensor.matmul(total[:], w21_sb[:], neighbours, start=(e == 0), stop=(e == DEGREE - 1))
 
-        for c, queue in zip(range(0, TARGETS, OUT_CHUNK), (nc.sync, nc.scalar)):
+        for c in range(0, TARGETS, OUT_CHUNK):
             leaky_affine(nc, work, out_sb[:, c : c + OUT_CHUNK], total[:, c : c + OUT_CHUNK], 1.0 / DEGREE, b21_sb)
-            queue.dma_start(out[:, c : c + OUT_CHUNK], out_sb[:, c : c + OUT_CHUNK])
+            nc.sync.dma_start(out[:, c : c + OUT_CHUNK], out_sb[:, c : c + OUT_CHUNK])

@@ -14,7 +14,6 @@ DEGREE = 16
 NEG_SLOPE = 0.2
 CHUNK = 128
 OUT_CHUNK = 256
-WARM_MATMULS = 12
 OFFSET_COLUMNS = TARGETS // 16
 
 FLOPS = 2 * P * P * (2 * NODES + DEGREE * TARGETS)
@@ -33,7 +32,6 @@ def tile_memlayer_kernel(tc, x_node, w1, b1, w2, b2, w21, b21, offs, out):
         tc.tile_pool(name="work", bufs=6) as work,
         tc.psum_pool(name="mlp_psum", bufs=6) as mlp_psum,
         tc.psum_pool(name="sum_psum", bufs=1) as sum_psum,
-        tc.psum_pool(name="warm_psum", bufs=1) as warm_psum,
     ):
         x_sb = held.tile([P, NODES], BF16)
         x1 = held.tile([P, NODES], BF16)
@@ -59,12 +57,6 @@ def tile_memlayer_kernel(tc, x_node, w1, b1, w2, b2, w21, b21, offs, out):
         nc.sync.dma_start(w21_sb[:], w21)
         nc.sync.dma_start(b21_sb[:], b21)
         nc.sync.dma_start(offsets[:], offs)
-
-        zeros = held.tile([P, P], BF16)
-        nc.vector.memset(zeros[:], 0.0)
-        unread = warm_psum.tile([P, P], F32)
-        for repeat in range(WARM_MATMULS):
-            nc.tensor.matmul(unread[:], zeros[:], zeros[:])
 
         one_column = held.tile([P, 1], F32)
         nc.vector.memset(one_column[:], 0.0)

@@ -29,7 +29,7 @@ def tile_memlayer_kernel(tc, x_node, w1, b1, w2, b2, w21, b21, offs, out):
     nc = tc.nc
     with (
         tc.tile_pool(name="held", bufs=1) as held,
-        tc.tile_pool(name="work", bufs=6) as work,
+        tc.tile_pool(name="work", bufs=18) as work,
         tc.psum_pool(name="mlp_psum", bufs=6) as mlp_psum,
         tc.psum_pool(name="sum_psum", bufs=1) as sum_psum,
     ):

@@ -14,6 +14,7 @@ DEGREE = 16
 NEG_SLOPE = 0.2
 CHUNK = 128
 OUT_CHUNK = 256
+HALF = NODES // 2
 OFFSET_COLUMNS = TARGETS // 16
 
 FLOPS = 2 * P * P * (2 * NODES + DEGREE * TARGETS)
@@ -48,15 +49,13 @@ def tile_memlayer_kernel(tc, x_node, w1, b1, w2, b2, w21, b21, offs, out):
         nc.sync.dma_start(w1_sb[:], w1)
         nc.sync.dma_start(x_sb[:, 0:CHUNK], x_node[:, 0:CHUNK])
         nc.sync.dma_start(b1_sb[:], b1)
-        loaded = CHUNK
-        while loaded < NODES:
-            nc.sync.dma_start(x_sb[:, loaded : 2 * loaded], x_node[:, loaded : 2 * loaded])
-            loaded = 2 * loaded
+        nc.sync.dma_start(x_sb[:, CHUNK:HALF], x_node[:, CHUNK:HALF])
+        nc.sync.dma_start(x_sb[:, HALF:NODES], x_node[:, HALF:NODES])
         nc.sync.dma_start(w2_sb[:], w2)
         nc.sync.dma_start(b2_sb[:], b2)
+        nc.sync.dma_start(offsets[:], offs)
         nc.sync.dma_start(w21_sb[:], w21)
         nc.sync.dma_start(b21_sb[:], b21)
-        nc.sync.dma_start(offsets[:], offs)
 
         one_column = held.tile([P, 1], F32)
         nc.vector.memset(one_column[:], 0.0)

@@ -14,7 +14,6 @@ DEGREE = 16
 NEG_SLOPE = 0.2
 CHUNK = 128
 OUT_CHUNK = 256
-HALF = NODES // 2
 OFFSET_COLUMNS = TARGETS // 16
 
 FLOPS = 2 * P * P * (2 * NODES + DEGREE * TARGETS)
@@ -49,8 +48,9 @@ def tile_memlayer_kernel(tc, x_node, w1, b1, w2, b2, w21, b21, offs, out):
         nc.sync.dma_start(w1_sb[:], w1)
         nc.sync.dma_start(x_sb[:, 0:CHUNK], x_node[:, 0:CHUNK])
         nc.sync.dma_start(b1_sb[:], b1)
-        nc.sync.dma_start(x_sb[:, CHUNK:HALF], x_node[:, CHUNK:HALF])
-        nc.sync.dma_start(x_sb[:, HALF:NODES], x_node[:, HALF:NODES])
+        nc.sync.dma_start(x_sb[:, CHUNK : 2 * CHUNK], x_node[:, CHUNK : 2 * CHUNK])
+        for c in range(2 * CHUNK, NODES, 2 * CHUNK):
+            nc.sync.dma_start(x_sb[:, c : c + 2 * CHUNK], x_node[:, c : c + 2 * CHUNK])
         nc.sync.dma_start(w2_sb[:], w2)
         nc.sync.dma_start(b2_sb[:], b2)
         nc.sync.dma_start(offsets[:], offs)

@@ -12,6 +12,7 @@ NODES = 1024
 TARGETS = 512
 DEGREE = 16
 NEG_SLOPE = 0.2
+WARM_UP = 12
 CHUNK = 128
 OUT_CHUNK = 256
 OFFSET_COLUMNS = TARGETS // 16
@@ -60,6 +61,12 @@ def tile_memlayer_kernel(tc, x_node, w1, b1, w2, b2, w21, b21, offs, out):
         one_column = held.tile([P, 1], F32)
         nc.vector.memset(one_column[:], 0.0)
         nc.scalar.activation(one_column[:], one_column[:], IDENTITY)
+
+        zeros = held.tile([P, P], BF16)
+        nc.vector.memset(zeros[:], 0.0)
+        unread = sum_psum.tile([P, P], F32)
+        for w in range(WARM_UP):
+            nc.tensor.matmul(unread[:], zeros[:], zeros[:])
 
         for source, weights, bias, dest in ((x_sb, w1_sb, b1_sb, x1), (x1, w2_sb, b2_sb, h)):
             for c in range(0, NODES, CHUNK):

@@ -14,6 +14,7 @@ DEGREE = 16
 NEG_SLOPE = 0.2
 WARM_UP = 12
 CHUNK = 128
+OUT_STEP = 128
 OUT_CHUNK = 256
 OFFSET_COLUMNS = TARGETS // 16
 
@@ -30,7 +31,7 @@ def tile_memlayer_kernel(tc, x_node, w1, b1, w2, b2, w21, b21, offs, out):
     nc = tc.nc
     with (
         tc.tile_pool(name="held", bufs=1) as held,
-        tc.tile_pool(name="work", bufs=18) as work,
+        tc.tile_pool(name="work", bufs=20) as work,
         tc.psum_pool(name="mlp_psum", bufs=6) as mlp_psum,
         tc.psum_pool(name="sum_psum", bufs=1) as sum_psum,
     ):
@@ -58,12 +59,11 @@ def tile_memlayer_kernel(tc, x_node, w1, b1, w2, b2, w21, b21, offs, out):
         nc.sync.dma_start(w21_sb[:], w21)
         nc.sync.dma_start(b21_sb[:], b21)
 
-        one_column = held.tile([P, 1], F32)
-        nc.vector.memset(one_column[:], 0.0)
-        nc.scalar.activation(one_column[:], one_column[:], IDENTITY)
-
         zeros = held.tile([P, P], BF16)
         nc.vector.memset(zeros[:], 0.0)
+        one_column = held.tile([P, 1], F32)
+        nc.scalar.activation(one_column[:], zeros[:, 0:1], IDENTITY)
+
         unread = sum_psum.tile([P, P], F32)
         for w in range(WARM_UP):
             nc.tensor.matmul(unread[:], zeros[:], zeros[:])
@@ -80,5 +80,6 @@ def tile_memlayer_kernel(tc, x_node, w1, b1, w2, b2, w21, b21, offs, out):
             nc.tensor.matmul(total[:], w21_sb[:], neighbours, start=(e == 0), stop=(e == DEGREE - 1))
 
         for c in range(0, TARGETS, OUT_CHUNK):
-            leaky_affine(nc, work, out_sb[:, c : c + OUT_CHUNK], total[:, c : c + OUT_CHUNK], 1.0 / DEGREE, b21_sb)
+            for s in range(c, c + OUT_CHUNK, OUT_STEP):
+                leaky_affine(nc, work, out_sb[:, s : s + OUT_STEP], total[:, s : s + OUT_STEP], 1.0 / DEGREE, b21_sb)
             nc.sync.dma_start(out[:, c : c + OUT_CHUNK], out_sb[:, c : c + OUT_CHUNK])

import concourse.mybir as mybir

BF16 = mybir.dt.bfloat16
F32 = mybir.dt.float32
U16 = mybir.dt.uint16
IDENTITY = mybir.ActivationFunctionType.Identity
MULT = mybir.AluOpType.mult
MAX = mybir.AluOpType.max

P = 128
NODES = 1024
TARGETS = 512
DEGREE = 16
NEG_SLOPE = 0.2
WARM_UP = 12
CHUNK = 128
OUT_STEP = 128
OUT_CHUNK = 256
OFFSET_COLUMNS = TARGETS // 16

FLOPS = 2 * P * P * (2 * NODES + DEGREE * TARGETS)


def leaky_affine(nc, work, dest, product, scale, bias):
    v = work.tile(list(product.shape), F32)
    nc.scalar.activation(v[:], product, IDENTITY, bias=bias[:], scale=scale)
    nc.vector.scalar_tensor_tensor(dest, v[:], NEG_SLOPE, v[:], MULT, MAX)


def tile_memlayer_kernel(tc, x_node, w1, b1, w2, b2, w21, b21, offs, out):
    nc = tc.nc
    with (
        tc.tile_pool(name="held", bufs=1) as held,
        tc.tile_pool(name="work", bufs=20) as work,
        tc.psum_pool(name="mlp_psum", bufs=6) as mlp_psum,
        tc.psum_pool(name="sum_psum", bufs=1) as sum_psum,
    ):
        x_sb = held.tile([P, NODES], BF16)
        x1 = held.tile([P, NODES], BF16)
        h = held.tile([P, NODES], BF16)
        w1_sb = held.tile([P, P], BF16)
        w2_sb = held.tile([P, P], BF16)
        w21_sb = held.tile([P, P], BF16)
        b1_sb = held.tile([P, 1], F32)
        b2_sb = held.tile([P, 1], F32)
        b21_sb = held.tile([P, 1], F32)
        offsets = held.tile([P, DEGREE * OFFSET_COLUMNS], U16)
        out_sb = held.tile([P, TARGETS], F32)

        nc.sync.dma_start(w1_sb[:], w1)
        nc.sync.dma_start(x_sb[:, 0:CHUNK], x_node[:, 0:CHUNK])
        nc.sync.dma_start(b1_sb[:], b1)
        nc.sync.dma_start(x_sb[:, CHUNK : 2 * CHUNK], x_node[:, CHUNK : 2 * CHUNK])
        for c in range(2 * CHUNK, NODES, 2 * CHUNK):
            nc.sync.dma_start(x_sb[:, c : c + 2 * CHUNK], x_node[:, c : c + 2 * CHUNK])
        nc.sync.dma_start(w2_sb[:], w2)
        nc.sync.dma_start(b2_sb[:], b2)
        nc.sync.dma_start(offsets[:], offs)
        nc.sync.dma_start(w21_sb[:], w21)
        nc.sync.dma_start(b21_sb[:], b21)

        zeros = held.tile([P, P], BF16)
        nc.vector.memset(zeros[:], 0.0)
        one_column = held.tile([P, 1], F32)
        nc.scalar.activation(one_column[:], zeros[:, 0:1], IDENTITY)

        unread = sum_psum.tile([P, P], F32)
        for w in range(WARM_UP):
            nc.tensor.matmul(unread[:], zeros[:], zeros[:])

        for source, weights, bias, dest in ((x_sb, w1_sb, b1_sb, x1), (x1, w2_sb, b2_sb, h)):
            for c in range(0, NODES, CHUNK):
                product = mlp_psum.tile([P, CHUNK], F32)
                nc.tensor.matmul(product[:], weights[:], source[:, c : c + CHUNK])
                leaky_affine(nc, work, dest[:, c : c + CHUNK], product[:], 1.0, bias)

        total = sum_psum.tile([P, TARGETS], F32)
        for e in range(DEGREE):
            neighbours = h[:].indirect(offsets[:, e * OFFSET_COLUMNS : (e + 1) * OFFSET_COLUMNS])
            nc.tensor.matmul(total[:], w21_sb[:], neighbours, start=(e == 0), stop=(e == DEGREE - 1))

        for c in range(0, TARGETS, OUT_CHUNK):
            for s in range(c, c + OUT_CHUNK, OUT_STEP):
                leaky_affine(nc, work, out_sb[:, s : s + OUT_STEP], total[:, s : s + OUT_STEP], 1.0 / DEGREE, b21_sb)
            nc.sync.dma_start(out[:, c : c + OUT_CHUNK], out_sb[:, c : c + OUT_CHUNK])
